import numpy as np
import ml_dtypes


def mxq(x, axis, fmt="e4m3"):
    dtype, down = {"e4m3": (ml_dtypes.float8_e4m3fn, 7), "e5m2": (ml_dtypes.float8_e5m2, 14)}[fmt]
    v = np.moveaxis(np.asarray(x, np.float32).astype(ml_dtypes.bfloat16).astype(np.float64), axis, -1)
    blocks = v.reshape(v.shape[:-1] + (-1, 32))
    amax = np.abs(blocks).max(-1, keepdims=True)
    byte = np.maximum(np.where(amax > 0, np.frexp(amax)[1] - 1 + 127, 0) - down, 1)
    scale = np.exp2(byte - 127.0)
    codes = (blocks / scale).astype(np.float32).astype(dtype).astype(np.float64)
    return np.moveaxis((codes * scale).reshape(v.shape), -1, axis)


WIDE = False


def mx_kscale(k):
    if not WIDE:
        return np.ones(k)
    levels = np.array([10, -10, 5, -5, 0])
    a = np.random.permutation(np.resize(levels, k // 512 * 4)).reshape(k // 512, 4)
    idx = np.arange(k)
    return np.exp2(a[idx // 512, idx % 128 // 32])


BF16 = ml_dtypes.bfloat16


def bf(x):
    return np.asarray(x, np.float32).astype(BF16)


def f64(x):
    return np.asarray(x).astype(np.float64)


E2M1 = np.array([0.0, 0.5, 1.0, 1.5, 2.0, 3.0, 4.0, 6.0, -0.0, -0.5, -1.0, -1.5, -2.0, -3.0, -4.0, -6.0])


def pack_weight(w, fmt):
    k, n = w.shape
    w = f64(bf(w)).reshape(k // 32, 32, n)
    amax = np.abs(w).max(1)
    if fmt == "e4m3":
        byte = np.frexp(amax)[1] - 1 + 127 - 7
    else:
        mant, ex = np.frexp(amax / 6.0)
        byte = np.where(mant > 0.5, ex, ex - 1) + 127
    byte = np.clip(np.where(amax > 0, byte, 1), 1, 254)
    scaled = (w * np.exp2(127.0 - byte)[:, None, :]).reshape(k, n).astype(np.float32)
    by_word = np.ascontiguousarray(scaled.reshape(k // 512, 128, 4, n).transpose(0, 1, 3, 2))
    if fmt == "e4m3":
        words = by_word.astype(ml_dtypes.float8_e4m3fn).view(np.uint8)
    else:
        c = by_word.astype(ml_dtypes.float4_e2m1fn).view(np.uint8) & 0xF
        words = c[..., 0::2] | (c[..., 1::2] << 4)
    return np.ascontiguousarray(words), np.ascontiguousarray(byte.astype(np.uint8).reshape(k // 512, 16, n))


def unpack_weight(words, scales, fmt):
    g, p, n, _ = words.shape
    if fmt == "e4m3":
        vals = np.ascontiguousarray(words).view(ml_dtypes.float8_e4m3fn).astype(np.float64)
    else:
        nib = np.empty((g, p, n, 4), np.uint8)
        nib[..., 0::2] = words & 0xF
        nib[..., 1::2] = words >> 4
        vals = E2M1[nib]
    vals = vals * np.repeat(np.exp2(scales.astype(np.float64) - 127.0), 8, axis=1)[..., None]
    return vals.transpose(0, 1, 3, 2).reshape(g * 512, n)

def pack4(w):
    words, scales = pack_weight(w, "e2m1")
    return words.reshape(words.shape[0], 128, -1), scales


def unpack4(words, scales):
    return unpack_weight(words.reshape(words.shape[0], 128, -1, 2), scales, "e2m1")


B, H, N, D, DT, NH = 8, 128, 128, 1024, 512, 8


def softmax(v, axis):
    e = np.exp(v - v.max(axis=axis, keepdims=True))
    return e / e.sum(axis=axis, keepdims=True)


def setup_inputs():
    s = mx_kscale(DT)
    cand_topics = bf(np.random.standard_normal((B, N, DT)) * s)
    Wq = np.random.standard_normal((D, DT)) * 2.0 / np.sqrt(DT) / s[None, :]
    Wq_words, Wq_scales = pack4(np.ascontiguousarray(Wq.T))
    bq = bf(np.random.standard_normal(D) * 0.5)
    return {"cand_topics": cand_topics,
            "Wq_words": Wq_words,
            "Wq_scales": Wq_scales,
            "bq": bq}


def reference(cand_topics, Wq_words, Wq_scales, bq):
    q = (mxq(f64(cand_topics), 2, "e4m3") @ unpack4(Wq_words, Wq_scales)) + f64(bq)
    query_weights = softmax(np.sqrt((q ** 2).sum(axis=-1)), 1)
    return q, query_weights

@@ -1,0 +1,164 @@
+from contextlib import ExitStack
+
+import concourse.mybir as mybir
+from concourse.masks import make_identity
+
+F32 = mybir.dt.float32
+BF16 = mybir.dt.bfloat16
+I32 = mybir.dt.int32
+U32 = mybir.dt.uint32
+U8 = mybir.dt.uint8
+FP8X4 = mybir.dt.float8_e4m3fn_x4
+FP4X4 = mybir.dt.float4_e2m1fn_x4
+ALU = mybir.AluOpType
+ACT = mybir.ActivationFunctionType
+
+P = 128
+USERS = 8
+K = 512
+FEATURES = 1024
+BANK = 512
+HALVES = FEATURES // BANK
+FIRST = 2
+RATE = 2
+
+FLOPS = 2 * USERS * P * K * FEATURES
+
+
+def tile_candidateaware_clickednewsattention_pa_kernel(
+    tc, cand_topics, Wq_words, Wq_scales, bq, out_0, out_1
+):
+    nc = tc.nc
+    with ExitStack() as ctx:
+        keep = ctx.enter_context(tc.tile_pool(name="keep", bufs=1))
+        q_pool = ctx.enter_context(tc.tile_pool(name="q_pool", bufs=USERS))
+        xt_pool = ctx.enter_context(tc.psum_pool(name="xt_pool", bufs=4))
+        acc_pool = ctx.enter_context(tc.psum_pool(name="acc_pool", bufs=2 * HALVES))
+        ctx.enter_context(tc.manual_schedule())
+
+        x_sb = keep.tile([P, USERS, K], BF16)
+        grouped = keep.tile([P, USERS, 4 * P], BF16, align_bytes=64)
+        x_codes = keep.tile([P, USERS, P], U32, align_bytes=64)
+        x_scales = keep.tile([P, USERS, P], U8, align_bytes=64)
+        w_words = keep.tile([P, 2 * FEATURES], U8, align_bytes=64)
+        w_scales = keep.tile([P, FEATURES], U8, align_bytes=64)
+        bias_rows = keep.tile([P, FEATURES], BF16)
+        bias_sb = keep.tile([P, FEATURES], BF16)
+        ones = keep.tile([P, P], BF16)
+        ident = keep.tile([P, P], F32)
+        warm = keep.tile([P, 1], F32)
+        half = keep.tile([P, 1], F32)
+        squares = keep.tile([P, FEATURES], F32)
+        sum_sq = keep.tile([P, USERS], F32)
+        norm_pad = keep.tile([P, P], F32)
+
+        nc.vector.memset(bias_rows[:], 0.0)
+        nc.vector.memset(w_scales[:].bitcast(I32), 0)
+        nc.vector.memset(warm[:], 0.0)
+        nc.vector.memset(ones[:], 1.0)
+        nc.vector.memset(half[:], 0.5)
+        nc.vector.memset(norm_pad[:], 0.0)
+        make_identity(nc, ident[:])
+        nc.scalar.activation(out=warm[:], in_=warm[:], func=ACT.Exp)
+
+        def load_users(first, last):
+            nc.sync.dma_start(
+                out=x_sb[:, first:last, :],
+                in_=cand_topics[first:last].rearrange("b n k -> n b k"),
+            )
+
+        load_users(0, FIRST)
+        nc.sync.dma_start(out=bias_rows[0:1, :], in_=bq.unsqueeze(0))
+        for quadrant in range(4):
+            nc.sync.dma_start(
+                out=w_scales[32 * quadrant : 32 * quadrant + 4, :].bitcast(I32),
+                in_=Wq_scales[0, 4 * quadrant : 4 * quadrant + 4, :].bitcast(I32),
+            )
+        nc.sync.dma_start(out=w_words[:].bitcast(I32), in_=Wq_words[0].bitcast(I32))
+        for first in range(FIRST, USERS, RATE):
+            load_users(first, first + RATE)
+
+        def transpose(b):
+            xt = xt_pool.tile([P, 2, P], F32, name="xt")
+            words = x_sb[:, b, :].bitcast(F32)
+            for u in range(2):
+                nc.tensor.transpose(xt[:, u, :], words[:, u : K // 2 : 2], ident[:])
+            return xt
+
+        def regroup(b, xt):
+            nc.scalar.copy(
+                out=grouped[:, b, :].bitcast(F32).rearrange("p (r u) -> p r u", u=2),
+                in_=xt[:].rearrange("p u r -> p r u"),
+            )
+
+        def quantise(b):
+            nc.vector.quantize_mx(
+                out=x_codes[:, b, :].bitcast(FP8X4),
+                scales=x_scales[:, b, :],
+                in_=grouped[:, b, :],
+            )
+
+        def multiply(b, h):
+            acc = acc_pool.tile([P, BANK], F32, name="acc")
+            nc.tensor.matmul_mx(
+                out=acc[:],
+                lhsT=x_codes[:, b, :].bitcast(FP8X4),
+                lhsT_scale=x_scales[:, b, :],
+                rhs=w_words[:, 2 * BANK * h : 2 * BANK * (h + 1)].bitcast(FP4X4),
+                rhs_scale=w_scales[:, BANK * h : BANK * (h + 1)],
+                start=True,
+                stop=True,
+            )
+            return acc
+
+        def add_bias_and_store(b, accs):
+            q_sb = q_pool.tile([P, FEATURES], F32, name="q_sb")
+            for h in range(HALVES):
+                cols = slice(BANK * h, BANK * (h + 1))
+                nc.vector.tensor_tensor(out=q_sb[:, cols], in0=accs[h][:], in1=bias_sb[:, cols], op=ALU.add)
+            nc.sync.dma_start(out=out_0[b], in_=q_sb[:])
+            return q_sb
+
+        def norm(b, q_sb):
+            nc.scalar.activation(
+                out=squares[:], in_=q_sb[:], func=ACT.Square, accum_out=sum_sq[:, b : b + 1]
+            )
+            nc.gpsimd.tensor_tensor(
+                out=norm_pad[:, b : b + 1], in0=sum_sq[:, b : b + 1], in1=half[:], op=ALU.pow
+            )
+
+        for b in range(FIRST):
+            regroup(b, transpose(b))
+            quantise(b)
+        bias_ps = xt_pool.tile([P, FEATURES], BF16, name="bias_ps", tag="xt")
+        for h in range(HALVES):
+            cols = slice(BANK * h, BANK * (h + 1))
+            nc.tensor.matmul(out=bias_ps[:, cols], lhsT=ones[:], rhs=bias_rows[:, cols], start=True, stop=True)
+        nc.scalar.copy(out=bias_sb[:], in_=bias_ps[:])
+
+        products = {0: [multiply(0, h) for h in range(HALVES)]}
+        regrouped = range(0)
+        for b in range(USERS):
+            for later in regrouped:
+                quantise(later)
+            regrouped = range(min(FIRST + RATE * b, USERS), min(FIRST + RATE * (b + 1), USERS))
+            for later in regrouped:
+                regroup(later, transpose(later))
+            if b + 1 < USERS:
+                products[b + 1] = [multiply(b + 1, h) for h in range(HALVES)]
+            q_sb = add_bias_and_store(b, products[b])
+            norm(b, q_sb)
+
+        norm_t = xt_pool.tile([P, 2, P], F32, name="xt")
+        norms = norm_t[:, 0, :]
+        nc.tensor.transpose(norms, norm_pad[:], ident[:])
+        neg_max = keep.tile([P, 1], F32)
+        expd = keep.tile([P, P], F32)
+        total = keep.tile([P, 1], F32)
+        inv_total = keep.tile([P, 1], F32)
+        weights = keep.tile([P, P], F32)
+        nc.vector.tensor_reduce(out=neg_max[:], in_=norms, axis=mybir.AxisListType.X, op=ALU.max, negate=True)
+        nc.scalar.activation(out=expd[:], in_=norms, func=ACT.Exp, bias=neg_max[:], accum_out=total[:])
+        nc.vector.reciprocal(out=inv_total[:], in_=total[:])
+        nc.vector.tensor_scalar_mul(out=weights[:], in0=expd[:], scalar1=inv_total[:])
+        nc.sync.dma_start(out=out_1, in_=weights[0:USERS, :])

@@ -22,6 +22,8 @@ HALVES = FEATURES // BANK
 FIRST = 2
 RATE = 2
 
+WARM_UPS = 4
+
 FLOPS = 2 * USERS * P * K * FEATURES
 
 
@@ -45,6 +47,7 @@ def tile_candidateaware_clickednewsattention_pa_kernel(
         bias_rows = keep.tile([P, FEATURES], BF16)
         bias_sb = keep.tile([P, FEATURES], BF16)
         ones = keep.tile([P, P], BF16)
+        idle_rhs = keep.tile([P, BANK], BF16)
         ident = keep.tile([P, P], F32)
         warm = keep.tile([P, 1], F32)
         half = keep.tile([P, 1], F32)
@@ -54,6 +57,7 @@ def tile_candidateaware_clickednewsattention_pa_kernel(
 
         nc.vector.memset(bias_rows[:], 0.0)
         nc.vector.memset(w_scales[:].bitcast(I32), 0)
+        nc.vector.memset(idle_rhs[:], 0.0)
         nc.vector.memset(warm[:], 0.0)
         nc.vector.memset(ones[:], 1.0)
         nc.vector.memset(half[:], 0.5)
@@ -126,6 +130,10 @@ def tile_candidateaware_clickednewsattention_pa_kernel(
             nc.gpsimd.tensor_tensor(
                 out=norm_pad[:, b : b + 1], in0=sum_sq[:, b : b + 1], in1=half[:], op=ALU.pow
             )
+
+        idle_ps = acc_pool.tile([P, BANK], F32, name="acc")
+        for i in range(WARM_UPS):
+            nc.tensor.matmul(out=idle_ps[:], lhsT=idle_rhs[:, 0:P], rhs=idle_rhs[:], start=True, stop=True)
 
         for b in range(FIRST):
             regroup(b, transpose(b))

@@ -47,7 +47,7 @@ def tile_candidateaware_clickednewsattention_pa_kernel(
         bias_rows = keep.tile([P, FEATURES], BF16)
         bias_sb = keep.tile([P, FEATURES], BF16)
         ones = keep.tile([P, P], BF16)
-        idle_rhs = keep.tile([P, BANK], BF16)
+        idle = keep.tile([P, P], F32)
         ident = keep.tile([P, P], F32)
         warm = keep.tile([P, 1], F32)
         half = keep.tile([P, 1], F32)
@@ -55,9 +55,9 @@ def tile_candidateaware_clickednewsattention_pa_kernel(
         sum_sq = keep.tile([P, USERS], F32)
         norm_pad = keep.tile([P, P], F32)
 
+        nc.vector.memset(idle[:], 0.0)
         nc.vector.memset(bias_rows[:], 0.0)
         nc.vector.memset(w_scales[:].bitcast(I32), 0)
-        nc.vector.memset(idle_rhs[:], 0.0)
         nc.vector.memset(warm[:], 0.0)
         nc.vector.memset(ones[:], 1.0)
         nc.vector.memset(half[:], 0.5)
@@ -133,7 +133,7 @@ def tile_candidateaware_clickednewsattention_pa_kernel(
 
         idle_ps = acc_pool.tile([P, BANK], F32, name="acc")
         for i in range(WARM_UPS):
-            nc.tensor.matmul(out=idle_ps[:], lhsT=idle_rhs[:, 0:P], rhs=idle_rhs[:], start=True, stop=True)
+            nc.tensor.matmul(out=idle_ps[:, 0:P], lhsT=idle[:], rhs=idle[:], start=True, stop=True)
 
         for b in range(FIRST):
             regroup(b, transpose(b))

@@ -52,7 +52,9 @@ def tile_candidateaware_clickednewsattention_pa_kernel(
         warm = keep.tile([P, 1], F32)
         half = keep.tile([P, 1], F32)
         squares = keep.tile([P, FEATURES], F32)
+        squares_v = keep.tile([P, BANK], F32)
         sum_sq = keep.tile([P, USERS], F32)
+        parts = keep.tile([P, HALVES], F32)
         norm_pad = keep.tile([P, P], F32)
 
         nc.vector.memset(idle[:], 0.0)
@@ -131,6 +133,19 @@ def tile_candidateaware_clickednewsattention_pa_kernel(
                 out=norm_pad[:, b : b + 1], in0=sum_sq[:, b : b + 1], in1=half[:], op=ALU.pow
             )
 
+        def norm_shared(b, q_sb):
+            nc.vector.scalar_tensor_tensor(
+                out=squares_v[:], in0=q_sb[:, 0:BANK], scalar=1.0, in1=q_sb[:, 0:BANK],
+                op0=ALU.mult, op1=ALU.mult, accum_out=parts[:, 0:1],
+            )
+            nc.scalar.activation(
+                out=squares[:, BANK:FEATURES], in_=q_sb[:, BANK:FEATURES], func=ACT.Square, accum_out=parts[:, 1:2]
+            )
+            nc.vector.tensor_tensor(out=sum_sq[:, b : b + 1], in0=parts[:, 0:1], in1=parts[:, 1:2], op=ALU.add)
+            nc.gpsimd.tensor_tensor(
+                out=norm_pad[:, b : b + 1], in0=sum_sq[:, b : b + 1], in1=half[:], op=ALU.pow
+            )
+
         idle_ps = acc_pool.tile([P, BANK], F32, name="acc")
         for i in range(WARM_UPS):
             nc.tensor.matmul(out=idle_ps[:, 0:P], lhsT=idle[:], rhs=idle[:], start=True, stop=True)
@@ -138,24 +153,26 @@ def tile_candidateaware_clickednewsattention_pa_kernel(
         for b in range(FIRST):
             regroup(b, transpose(b))
             quantise(b)
-        bias_ps = xt_pool.tile([P, FEATURES], BF16, name="bias_ps", tag="xt")
         for h in range(HALVES):
             cols = slice(BANK * h, BANK * (h + 1))
-            nc.tensor.matmul(out=bias_ps[:, cols], lhsT=ones[:], rhs=bias_rows[:, cols], start=True, stop=True)
-        nc.scalar.copy(out=bias_sb[:], in_=bias_ps[:])
+            bias_ps = xt_pool.tile([P, BANK], BF16, name="bias_ps", tag="xt")
+            nc.tensor.matmul(out=bias_ps[:], lhsT=ones[:], rhs=bias_rows[:, cols], start=True, stop=True)
+            nc.scalar.copy(out=bias_sb[:, cols], in_=bias_ps[:])
 
         products = {0: [multiply(0, h) for h in range(HALVES)]}
-        regrouped = range(0)
         for b in range(USERS):
-            for later in regrouped:
-                quantise(later)
-            regrouped = range(min(FIRST + RATE * b, USERS), min(FIRST + RATE * (b + 1), USERS))
-            for later in regrouped:
+            if FIRST <= b + 1 < USERS and (b + 1 - FIRST) % RATE == 0:
+                for later in range(b + 1, b + 1 + RATE):
+                    quantise(later)
+            for later in range(min(FIRST + RATE * b, USERS), min(FIRST + RATE * (b + 1), USERS)):
                 regroup(later, transpose(later))
             if b + 1 < USERS:
                 products[b + 1] = [multiply(b + 1, h) for h in range(HALVES)]
             q_sb = add_bias_and_store(b, products[b])
-            norm(b, q_sb)
+            if b + 1 < USERS:
+                norm(b, q_sb)
+            else:
+                norm_shared(b, q_sb)
 
         norm_t = xt_pool.tile([P, 2, P], F32, name="xt")
         norms = norm_t[:, 0, :]

@@ -22,6 +22,7 @@ HALVES = FEATURES // BANK
 FIRST = 2
 RATE = 2
 
+KEPT_WARM = 2
 WARM_UPS = 4
 
 FLOPS = 2 * USERS * P * K * FEATURES
@@ -160,7 +161,10 @@ def tile_candidateaware_clickednewsattention_pa_kernel(
             nc.scalar.copy(out=bias_sb[:, cols], in_=bias_ps[:])
 
         products = {0: [multiply(0, h) for h in range(HALVES)]}
+        idle_tail = None
         for b in range(USERS):
+            if b == USERS - KEPT_WARM:
+                idle_tail = xt_pool.tile([P, 2, P], F32, name="xt")[:, 0, :]
             if FIRST <= b + 1 < USERS and (b + 1 - FIRST) % RATE == 0:
                 for later in range(b + 1, b + 1 + RATE):
                     quantise(later)
@@ -169,6 +173,11 @@ def tile_candidateaware_clickednewsattention_pa_kernel(
             if b + 1 < USERS:
                 products[b + 1] = [multiply(b + 1, h) for h in range(HALVES)]
             q_sb = add_bias_and_store(b, products[b])
+            if b >= USERS - KEPT_WARM:
+                for h in range(HALVES):
+                    nc.tensor.matmul(
+                        out=idle_tail[:, 0:P], lhsT=idle[:], rhs=q_sb[:, BANK * h : BANK * h + P], start=True, stop=True
+                    )
             if b + 1 < USERS:
                 norm(b, q_sb)
             else:

@@ -53,19 +53,19 @@ def tile_candidateaware_clickednewsattention_pa_kernel(
         warm = keep.tile([P, 1], F32)
         half = keep.tile([P, 1], F32)
         squares = keep.tile([P, FEATURES], F32)
-        squares_v = keep.tile([P, BANK], F32)
+        squares_v = keep.tile([P, FEATURES], F32)
         sum_sq = keep.tile([P, USERS], F32)
-        parts = keep.tile([P, HALVES], F32)
         norm_pad = keep.tile([P, P], F32)
 
         nc.vector.memset(idle[:], 0.0)
-        nc.vector.memset(bias_rows[:], 0.0)
-        nc.vector.memset(w_scales[:].bitcast(I32), 0)
+        nc.vector.memset(bias_rows[:].bitcast(I32), 0)
+        nc.gpsimd.memset(w_scales[:].bitcast(F32), 0.0)
         nc.vector.memset(warm[:], 0.0)
         nc.vector.memset(ones[:], 1.0)
         nc.vector.memset(half[:], 0.5)
         nc.vector.memset(norm_pad[:], 0.0)
         make_identity(nc, ident[:])
+        nc.scalar.dma_start(out=bias_rows[0:1, :], in_=bq.unsqueeze(0))
         nc.scalar.activation(out=warm[:], in_=warm[:], func=ACT.Exp)
 
         def load_users(first, last):
@@ -75,7 +75,6 @@ def tile_candidateaware_clickednewsattention_pa_kernel(
             )
 
         load_users(0, FIRST)
-        nc.sync.dma_start(out=bias_rows[0:1, :], in_=bq.unsqueeze(0))
         for quadrant in range(4):
             nc.sync.dma_start(
                 out=w_scales[32 * quadrant : 32 * quadrant + 4, :].bitcast(I32),
@@ -134,15 +133,11 @@ def tile_candidateaware_clickednewsattention_pa_kernel(
                 out=norm_pad[:, b : b + 1], in0=sum_sq[:, b : b + 1], in1=half[:], op=ALU.pow
             )
 
-        def norm_shared(b, q_sb):
+        def norm_last(b, q_sb):
             nc.vector.scalar_tensor_tensor(
-                out=squares_v[:], in0=q_sb[:, 0:BANK], scalar=1.0, in1=q_sb[:, 0:BANK],
-                op0=ALU.mult, op1=ALU.mult, accum_out=parts[:, 0:1],
+                out=squares_v[:], in0=q_sb[:], scalar=1.0, in1=q_sb[:],
+                op0=ALU.mult, op1=ALU.mult, accum_out=sum_sq[:, b : b + 1],
             )
-            nc.scalar.activation(
-                out=squares[:, BANK:FEATURES], in_=q_sb[:, BANK:FEATURES], func=ACT.Square, accum_out=parts[:, 1:2]
-            )
-            nc.vector.tensor_tensor(out=sum_sq[:, b : b + 1], in0=parts[:, 0:1], in1=parts[:, 1:2], op=ALU.add)
             nc.gpsimd.tensor_tensor(
                 out=norm_pad[:, b : b + 1], in0=sum_sq[:, b : b + 1], in1=half[:], op=ALU.pow
             )
@@ -153,12 +148,16 @@ def tile_candidateaware_clickednewsattention_pa_kernel(
 
         for b in range(FIRST):
             regroup(b, transpose(b))
-            quantise(b)
+        bias_ps = []
         for h in range(HALVES):
             cols = slice(BANK * h, BANK * (h + 1))
-            bias_ps = xt_pool.tile([P, BANK], BF16, name="bias_ps", tag="xt")
-            nc.tensor.matmul(out=bias_ps[:], lhsT=ones[:], rhs=bias_rows[:, cols], start=True, stop=True)
-            nc.scalar.copy(out=bias_sb[:, cols], in_=bias_ps[:])
+            half_ps = xt_pool.tile([P, BANK], BF16, name="bias_ps", tag="xt")
+            nc.tensor.matmul(out=half_ps[:], lhsT=ones[:], rhs=bias_rows[:, cols], start=True, stop=True)
+            bias_ps.append(half_ps)
+        quantise(0)
+        nc.vector.tensor_copy(out=bias_sb[:, 0:BANK], in_=bias_ps[0][:])
+        nc.scalar.copy(out=bias_sb[:, BANK:FEATURES], in_=bias_ps[1][:])
+        quantise(1)
 
         products = {0: [multiply(0, h) for h in range(HALVES)]}
         idle_tail = None
@@ -181,7 +180,7 @@ def tile_candidateaware_clickednewsattention_pa_kernel(
             if b + 1 < USERS:
                 norm(b, q_sb)
             else:
-                norm_shared(b, q_sb)
+                norm_last(b, q_sb)
 
         norm_t = xt_pool.tile([P, 2, P], F32, name="xt")
         norms = norm_t[:, 0, :]

@@ -23,6 +23,7 @@ FIRST = 2
 RATE = 2
 
 KEPT_WARM = 2
+ROOTS = {4: (0, 5), 5: (5, 6), 7: (6, 8)}
 WARM_UPS = 4
 
 FLOPS = 2 * USERS * P * K * FEATURES
@@ -51,7 +52,7 @@ def tile_candidateaware_clickednewsattention_pa_kernel(
         idle = keep.tile([P, P], F32)
         ident = keep.tile([P, P], F32)
         warm = keep.tile([P, 1], F32)
-        half = keep.tile([P, 1], F32)
+        half = keep.tile([P, USERS], F32)
         squares = keep.tile([P, FEATURES], F32)
         squares_v = keep.tile([P, FEATURES], F32)
         sum_sq = keep.tile([P, USERS], F32)
@@ -129,17 +130,17 @@ def tile_candidateaware_clickednewsattention_pa_kernel(
             nc.scalar.activation(
                 out=squares[:], in_=q_sb[:], func=ACT.Square, accum_out=sum_sq[:, b : b + 1]
             )
-            nc.gpsimd.tensor_tensor(
-                out=norm_pad[:, b : b + 1], in0=sum_sq[:, b : b + 1], in1=half[:], op=ALU.pow
-            )
 
         def norm_last(b, q_sb):
             nc.vector.scalar_tensor_tensor(
                 out=squares_v[:], in0=q_sb[:], scalar=1.0, in1=q_sb[:],
                 op0=ALU.mult, op1=ALU.mult, accum_out=sum_sq[:, b : b + 1],
             )
+
+        def roots(first, last):
+            users = slice(first, last)
             nc.gpsimd.tensor_tensor(
-                out=norm_pad[:, b : b + 1], in0=sum_sq[:, b : b + 1], in1=half[:], op=ALU.pow
+                out=norm_pad[:, users], in0=sum_sq[:, users], in1=half[:, users], op=ALU.pow
             )
 
         idle_ps = acc_pool.tile([P, BANK], F32, name="acc")
@@ -181,6 +182,8 @@ def tile_candidateaware_clickednewsattention_pa_kernel(
                 norm(b, q_sb)
             else:
                 norm_last(b, q_sb)
+            if b in ROOTS:
+                roots(*ROOTS[b])
 
         norm_t = xt_pool.tile([P, 2, P], F32, name="xt")
         norms = norm_t[:, 0, :]

@@ -36,6 +36,7 @@ def tile_candidateaware_clickednewsattention_pa_kernel(
     with ExitStack() as ctx:
         keep = ctx.enter_context(tc.tile_pool(name="keep", bufs=1))
         q_pool = ctx.enter_context(tc.tile_pool(name="q_pool", bufs=USERS))
+        squares_pool = ctx.enter_context(tc.tile_pool(name="squares_pool", bufs=3))
         xt_pool = ctx.enter_context(tc.psum_pool(name="xt_pool", bufs=4))
         acc_pool = ctx.enter_context(tc.psum_pool(name="acc_pool", bufs=2 * HALVES))
         ctx.enter_context(tc.manual_schedule())
@@ -53,7 +54,6 @@ def tile_candidateaware_clickednewsattention_pa_kernel(
         ident = keep.tile([P, P], F32)
         warm = keep.tile([P, 1], F32)
         half = keep.tile([P, USERS], F32)
-        squares = keep.tile([P, FEATURES], F32)
         squares_v = keep.tile([P, FEATURES], F32)
         sum_sq = keep.tile([P, USERS], F32)
         norm_pad = keep.tile([P, P], F32)
@@ -127,6 +127,7 @@ def tile_candidateaware_clickednewsattention_pa_kernel(
             return q_sb
 
         def norm(b, q_sb):
+            squares = squares_pool.tile([P, FEATURES], F32, name="squares")
             nc.scalar.activation(
                 out=squares[:], in_=q_sb[:], func=ACT.Square, accum_out=sum_sq[:, b : b + 1]
             )

@@ -23,7 +23,7 @@ FIRST = 2
 RATE = 2
 
 KEPT_WARM = 2
-ROOTS = {4: (0, 5), 5: (5, 6), 7: (6, 8)}
+ROOTS = {3: (0, 4), 4: (4, 5), 5: (5, 6), 7: (6, 8)}
 WARM_UPS = 4
 
 FLOPS = 2 * USERS * P * K * FEATURES

@@ -59,14 +59,14 @@ def tile_candidateaware_clickednewsattention_pa_kernel(
         norm_pad = keep.tile([P, P], F32)
 
         nc.vector.memset(idle[:], 0.0)
-        nc.vector.memset(bias_rows[:].bitcast(I32), 0)
-        nc.gpsimd.memset(w_scales[:].bitcast(F32), 0.0)
+        nc.vector.memset(w_scales[:].bitcast(I32), 0)
+        nc.vector.memset(bias_rows[0 : P - 1, :].bitcast(I32), 0)
         nc.vector.memset(warm[:], 0.0)
         nc.vector.memset(ones[:], 1.0)
         nc.vector.memset(half[:], 0.5)
         nc.vector.memset(norm_pad[:], 0.0)
         make_identity(nc, ident[:])
-        nc.scalar.dma_start(out=bias_rows[0:1, :], in_=bq.unsqueeze(0))
+        nc.scalar.dma_start(out=bias_rows[P - 1 : P, :], in_=bq.unsqueeze(0))
         nc.scalar.activation(out=warm[:], in_=warm[:], func=ACT.Exp)
 
         def load_users(first, last):
@@ -91,6 +91,27 @@ def tile_candidateaware_clickednewsattention_pa_kernel(
             for u in range(2):
                 nc.tensor.transpose(xt[:, u, :], words[:, u : K // 2 : 2], ident[:])
             return xt
+
+        def transpose_pair(b):
+            xt = xt_pool.tile([P, 2, 2, P], F32, name="xt")
+            for user in range(2):
+                words = x_sb[:, b + user, :].bitcast(F32)
+                for u in range(2):
+                    nc.tensor.transpose(xt[:, user, u, :], words[:, u : K // 2 : 2], ident[:])
+            return xt
+
+        def regroup_pair(b, xt):
+            nc.scalar.copy(
+                out=grouped[:, b : b + 2, :].bitcast(F32).rearrange("p b (r u) -> p b r u", u=2),
+                in_=xt[:].rearrange("p b u r -> p b r u"),
+            )
+
+        def quantise_pair(b):
+            nc.vector.quantize_mx(
+                out=x_codes[:, b : b + 2, :].rearrange("p b r -> p (b r)").bitcast(FP8X4),
+                scales=x_scales[:, b : b + 2, :].rearrange("p b r -> p (b r)"),
+                in_=grouped[:, b : b + 2, :].rearrange("p b k -> p (b k)"),
+            )
 
         def regroup(b, xt):
             nc.scalar.copy(
@@ -167,10 +188,17 @@ def tile_candidateaware_clickednewsattention_pa_kernel(
             if b == USERS - KEPT_WARM:
                 idle_tail = xt_pool.tile([P, 2, P], F32, name="xt")[:, 0, :]
             if FIRST <= b + 1 < USERS and (b + 1 - FIRST) % RATE == 0:
-                for later in range(b + 1, b + 1 + RATE):
-                    quantise(later)
-            for later in range(min(FIRST + RATE * b, USERS), min(FIRST + RATE * (b + 1), USERS)):
-                regroup(later, transpose(later))
+                if b == 1:
+                    for later in range(b + 1, b + 1 + RATE):
+                        quantise(later)
+                else:
+                    quantise_pair(b + 1)
+            if b == 0:
+                for later in range(FIRST, FIRST + RATE):
+                    regroup(later, transpose(later))
+            elif FIRST + RATE * b < USERS:
+                later = FIRST + RATE * b
+                regroup_pair(later, transpose_pair(later))
             if b + 1 < USERS:
                 products[b + 1] = [multiply(b + 1, h) for h in range(HALVES)]
             q_sb = add_bias_and_store(b, products[b])

@@ -23,6 +23,8 @@ FIRST = 2
 RATE = 2
 
 KEPT_WARM = 2
+PREPARED = {0: slice(2, 3), 1: slice(4, 6), 2: slice(6, 8)}
+QUANTISED = {1: slice(2, 3), 2: slice(3, 4), 3: slice(4, 6), 5: slice(6, 8)}
 ROOTS = {3: (0, 4), 4: (4, 5), 5: (5, 6), 7: (6, 8)}
 WARM_UPS = 4
 
@@ -54,8 +56,10 @@ def tile_candidateaware_clickednewsattention_pa_kernel(
         ident = keep.tile([P, P], F32)
         warm = keep.tile([P, 1], F32)
         half = keep.tile([P, USERS], F32)
+        parts = keep.tile([P, HALVES], F32)
         squares_v = keep.tile([P, FEATURES], F32)
-        sum_sq = keep.tile([P, USERS], F32)
+        sum_early = keep.tile([P, USERS // 2], F32)
+        sum_late = keep.tile([P, USERS // 2], F32)
         norm_pad = keep.tile([P, P], F32)
 
         nc.vector.memset(idle[:], 0.0)
@@ -85,45 +89,25 @@ def tile_candidateaware_clickednewsattention_pa_kernel(
         for first in range(FIRST, USERS, RATE):
             load_users(first, first + RATE)
 
-        def transpose(b):
-            xt = xt_pool.tile([P, 2, P], F32, name="xt")
-            words = x_sb[:, b, :].bitcast(F32)
-            for u in range(2):
-                nc.tensor.transpose(xt[:, u, :], words[:, u : K // 2 : 2], ident[:])
-            return xt
-
-        def transpose_pair(b):
-            xt = xt_pool.tile([P, 2, 2, P], F32, name="xt")
-            for user in range(2):
-                words = x_sb[:, b + user, :].bitcast(F32)
+        def transpose(users):
+            xt = xt_pool.tile([P, users.stop - users.start, 2, P], F32, name="xt")
+            for b in range(users.start, users.stop):
+                words = x_sb[:, b, :].bitcast(F32)
                 for u in range(2):
-                    nc.tensor.transpose(xt[:, user, u, :], words[:, u : K // 2 : 2], ident[:])
+                    nc.tensor.transpose(xt[:, b - users.start, u, :], words[:, u : K // 2 : 2], ident[:])
             return xt
 
-        def regroup_pair(b, xt):
+        def regroup(users, xt):
             nc.scalar.copy(
-                out=grouped[:, b : b + 2, :].bitcast(F32).rearrange("p b (r u) -> p b r u", u=2),
+                out=grouped[:, users, :].bitcast(F32).rearrange("p b (r u) -> p b r u", u=2),
                 in_=xt[:].rearrange("p b u r -> p b r u"),
             )
 
-        def quantise_pair(b):
+        def quantise(users):
             nc.vector.quantize_mx(
-                out=x_codes[:, b : b + 2, :].rearrange("p b r -> p (b r)").bitcast(FP8X4),
-                scales=x_scales[:, b : b + 2, :].rearrange("p b r -> p (b r)"),
-                in_=grouped[:, b : b + 2, :].rearrange("p b k -> p (b k)"),
-            )
-
-        def regroup(b, xt):
-            nc.scalar.copy(
-                out=grouped[:, b, :].bitcast(F32).rearrange("p (r u) -> p r u", u=2),
-                in_=xt[:].rearrange("p u r -> p r u"),
-            )
-
-        def quantise(b):
-            nc.vector.quantize_mx(
-                out=x_codes[:, b, :].bitcast(FP8X4),
-                scales=x_scales[:, b, :],
-                in_=grouped[:, b, :],
+                out=x_codes[:, users, :].rearrange("p b r -> p (b r)").bitcast(FP8X4),
+                scales=x_scales[:, users, :].rearrange("p b r -> p (b r)"),
+                in_=grouped[:, users, :].rearrange("p b k -> p (b k)"),
             )
 
         def multiply(b, h):
@@ -139,30 +123,29 @@ def tile_candidateaware_clickednewsattention_pa_kernel(
             )
             return acc
 
-        def add_bias_and_store(b, accs):
-            q_sb = q_pool.tile([P, FEATURES], F32, name="q_sb")
-            for h in range(HALVES):
-                cols = slice(BANK * h, BANK * (h + 1))
-                nc.vector.tensor_tensor(out=q_sb[:, cols], in0=accs[h][:], in1=bias_sb[:, cols], op=ALU.add)
-            nc.sync.dma_start(out=out_0[b], in_=q_sb[:])
-            return q_sb
+        def add_bias(h, acc, q_sb):
+            cols = slice(BANK * h, BANK * (h + 1))
+            nc.vector.tensor_tensor(out=q_sb[:, cols], in0=acc[:], in1=bias_sb[:, cols], op=ALU.add)
 
-        def norm(b, q_sb):
+        def sum_squares(q_sb, cols, total):
             squares = squares_pool.tile([P, FEATURES], F32, name="squares")
-            nc.scalar.activation(
-                out=squares[:], in_=q_sb[:], func=ACT.Square, accum_out=sum_sq[:, b : b + 1]
-            )
+            nc.scalar.activation(out=squares[:, cols], in_=q_sb[:, cols], func=ACT.Square, accum_out=total)
 
-        def norm_last(b, q_sb):
+        def sum_squares_on_vector(q_sb, total):
             nc.vector.scalar_tensor_tensor(
                 out=squares_v[:], in0=q_sb[:], scalar=1.0, in1=q_sb[:],
-                op0=ALU.mult, op1=ALU.mult, accum_out=sum_sq[:, b : b + 1],
+                op0=ALU.mult, op1=ALU.mult, accum_out=total,
             )
+
+        def sums(first, last):
+            tile = sum_early if first < USERS // 2 else sum_late
+            start = first % (USERS // 2)
+            return tile[:, start : start + last - first]
 
         def roots(first, last):
             users = slice(first, last)
             nc.gpsimd.tensor_tensor(
-                out=norm_pad[:, users], in0=sum_sq[:, users], in1=half[:, users], op=ALU.pow
+                out=norm_pad[:, users], in0=sums(first, last), in1=half[:, users], op=ALU.pow
             )
 
         idle_ps = acc_pool.tile([P, BANK], F32, name="acc")
@@ -170,47 +153,50 @@ def tile_candidateaware_clickednewsattention_pa_kernel(
             nc.tensor.matmul(out=idle_ps[:, 0:P], lhsT=idle[:], rhs=idle[:], start=True, stop=True)
 
         for b in range(FIRST):
-            regroup(b, transpose(b))
+            regroup(slice(b, b + 1), transpose(slice(b, b + 1)))
         bias_ps = []
         for h in range(HALVES):
             cols = slice(BANK * h, BANK * (h + 1))
             half_ps = xt_pool.tile([P, BANK], BF16, name="bias_ps", tag="xt")
             nc.tensor.matmul(out=half_ps[:], lhsT=ones[:], rhs=bias_rows[:, cols], start=True, stop=True)
             bias_ps.append(half_ps)
-        quantise(0)
+        quantise(slice(0, 1))
         nc.vector.tensor_copy(out=bias_sb[:, 0:BANK], in_=bias_ps[0][:])
         nc.scalar.copy(out=bias_sb[:, BANK:FEATURES], in_=bias_ps[1][:])
-        quantise(1)
+        quantise(slice(1, 2))
 
         products = {0: [multiply(0, h) for h in range(HALVES)]}
+        held = None
         idle_tail = None
         for b in range(USERS):
             if b == USERS - KEPT_WARM:
                 idle_tail = xt_pool.tile([P, 2, P], F32, name="xt")[:, 0, :]
-            if FIRST <= b + 1 < USERS and (b + 1 - FIRST) % RATE == 0:
-                if b == 1:
-                    for later in range(b + 1, b + 1 + RATE):
-                        quantise(later)
-                else:
-                    quantise_pair(b + 1)
-            if b == 0:
-                for later in range(FIRST, FIRST + RATE):
-                    regroup(later, transpose(later))
-            elif FIRST + RATE * b < USERS:
-                later = FIRST + RATE * b
-                regroup_pair(later, transpose_pair(later))
+            q_sb = q_pool.tile([P, FEATURES], F32, name="q_sb")
+            if b in QUANTISED:
+                quantise(QUANTISED[b])
+            if b in PREPARED:
+                regroup(PREPARED[b], transpose(PREPARED[b]))
+            add_bias(0, products[b][0], q_sb)
             if b + 1 < USERS:
                 products[b + 1] = [multiply(b + 1, h) for h in range(HALVES)]
-            q_sb = add_bias_and_store(b, products[b])
+            add_bias(1, products[b][1], q_sb)
+            nc.sync.dma_start(out=out_0[b], in_=q_sb[:])
             if b >= USERS - KEPT_WARM:
                 for h in range(HALVES):
                     nc.tensor.matmul(
                         out=idle_tail[:, 0:P], lhsT=idle[:], rhs=q_sb[:, BANK * h : BANK * h + P], start=True, stop=True
                     )
-            if b + 1 < USERS:
-                norm(b, q_sb)
+            if b == 0:
+                sum_squares(q_sb, slice(0, BANK), parts[:, 0:1])
+                regroup(slice(3, 4), transpose(slice(3, 4)))
+                sum_squares(q_sb, slice(BANK, FEATURES), parts[:, 1:2])
+                nc.gpsimd.tensor_tensor(out=sums(0, 1), in0=parts[:, 0:1], in1=parts[:, 1:2], op=ALU.add)
+            elif b == USERS - 2:
+                held = q_sb
             else:
-                norm_last(b, q_sb)
+                sum_squares(q_sb, slice(0, FEATURES), sums(b, b + 1))
+            if b == USERS - 1:
+                sum_squares_on_vector(held, sums(b - 1, b))
             if b in ROOTS:
                 roots(*ROOTS[b])
 

@@ -23,6 +23,7 @@ FIRST = 2
 RATE = 2
 
 KEPT_WARM = 2
+RELIEVED = 2
 PREPARED = {0: slice(2, 3), 1: slice(4, 6), 2: slice(6, 8)}
 QUANTISED = {1: slice(2, 3), 2: slice(3, 4), 3: slice(4, 6), 5: slice(6, 8)}
 ROOTS = {3: (0, 4), 4: (4, 5), 5: (5, 6), 7: (6, 8)}
@@ -57,6 +58,7 @@ def tile_candidateaware_clickednewsattention_pa_kernel(
         warm = keep.tile([P, 1], F32)
         half = keep.tile([P, USERS], F32)
         parts = keep.tile([P, HALVES], F32)
+        y_half = keep.tile([P, BANK], F32)
         squares_v = keep.tile([P, FEATURES], F32)
         sum_early = keep.tile([P, USERS // 2], F32)
         sum_late = keep.tile([P, USERS // 2], F32)
@@ -174,12 +176,20 @@ def tile_candidateaware_clickednewsattention_pa_kernel(
             q_sb = q_pool.tile([P, FEATURES], F32, name="q_sb")
             if b in QUANTISED:
                 quantise(QUANTISED[b])
-            if b in PREPARED:
+            if b in PREPARED and b != RELIEVED:
                 regroup(PREPARED[b], transpose(PREPARED[b]))
             add_bias(0, products[b][0], q_sb)
             if b + 1 < USERS:
                 products[b + 1] = [multiply(b + 1, h) for h in range(HALVES)]
-            add_bias(1, products[b][1], q_sb)
+            if b == RELIEVED:
+                regroup(PREPARED[b], transpose(PREPARED[b]))
+            if b + 1 == RELIEVED:
+                nc.scalar.copy(out=y_half[:], in_=products[b + 1][1][:])
+            if b == RELIEVED:
+                cols = slice(BANK, FEATURES)
+                nc.gpsimd.tensor_tensor(out=q_sb[:, cols], in0=y_half[:], in1=bias_sb[:, cols], op=ALU.add)
+            else:
+                add_bias(1, products[b][1], q_sb)
             nc.sync.dma_start(out=out_0[b], in_=q_sb[:])
             if b >= USERS - KEPT_WARM:
                 for h in range(HALVES):

@@ -26,8 +26,8 @@ KEPT_WARM = 2
 RELIEVED = 2
 PREPARED = {0: slice(2, 3), 1: slice(4, 6), 2: slice(6, 8)}
 QUANTISED = {1: slice(2, 3), 2: slice(3, 4), 3: slice(4, 6), 5: slice(6, 8)}
-ROOTS = {3: (0, 4), 4: (4, 5), 5: (5, 6), 7: (6, 8)}
-WARM_UPS = 4
+ROOTS = {2: (0, 3), 3: (3, 4), 4: (4, 5), 5: (5, 6), 7: (6, 8)}
+WARM_UPS = 3
 
 FLOPS = 2 * USERS * P * K * FEATURES
 

from contextlib import ExitStack

import concourse.mybir as mybir
from concourse.masks import make_identity

F32 = mybir.dt.float32
BF16 = mybir.dt.bfloat16
I32 = mybir.dt.int32
U32 = mybir.dt.uint32
U8 = mybir.dt.uint8
FP8X4 = mybir.dt.float8_e4m3fn_x4
FP4X4 = mybir.dt.float4_e2m1fn_x4
ALU = mybir.AluOpType
ACT = mybir.ActivationFunctionType

P = 128
USERS = 8
K = 512
FEATURES = 1024
BANK = 512
HALVES = FEATURES // BANK
FIRST = 2
RATE = 2

KEPT_WARM = 2
RELIEVED = 2
PREPARED = {0: slice(2, 3), 1: slice(4, 6), 2: slice(6, 8)}
QUANTISED = {1: slice(2, 3), 2: slice(3, 4), 3: slice(4, 6), 5: slice(6, 8)}
ROOTS = {2: (0, 3), 3: (3, 4), 4: (4, 5), 5: (5, 6), 7: (6, 8)}
WARM_UPS = 3

FLOPS = 2 * USERS * P * K * FEATURES


def tile_candidateaware_clickednewsattention_pa_kernel(
    tc, cand_topics, Wq_words, Wq_scales, bq, out_0, out_1
):
    nc = tc.nc
    with ExitStack() as ctx:
        keep = ctx.enter_context(tc.tile_pool(name="keep", bufs=1))
        q_pool = ctx.enter_context(tc.tile_pool(name="q_pool", bufs=USERS))
        squares_pool = ctx.enter_context(tc.tile_pool(name="squares_pool", bufs=3))
        xt_pool = ctx.enter_context(tc.psum_pool(name="xt_pool", bufs=4))
        acc_pool = ctx.enter_context(tc.psum_pool(name="acc_pool", bufs=2 * HALVES))
        ctx.enter_context(tc.manual_schedule())

        x_sb = keep.tile([P, USERS, K], BF16)
        grouped = keep.tile([P, USERS, 4 * P], BF16, align_bytes=64)
        x_codes = keep.tile([P, USERS, P], U32, align_bytes=64)
        x_scales = keep.tile([P, USERS, P], U8, align_bytes=64)
        w_words = keep.tile([P, 2 * FEATURES], U8, align_bytes=64)
        w_scales = keep.tile([P, FEATURES], U8, align_bytes=64)
        bias_rows = keep.tile([P, FEATURES], BF16)
        bias_sb = keep.tile([P, FEATURES], BF16)
        ones = keep.tile([P, P], BF16)
        idle = keep.tile([P, P], F32)
        ident = keep.tile([P, P], F32)
        warm = keep.tile([P, 1], F32)
        half = keep.tile([P, USERS], F32)
        parts = keep.tile([P, HALVES], F32)
        y_half = keep.tile([P, BANK], F32)
        squares_v = keep.tile([P, FEATURES], F32)
        sum_early = keep.tile([P, USERS // 2], F32)
        sum_late = keep.tile([P, USERS // 2], F32)
        norm_pad = keep.tile([P, P], F32)

        nc.vector.memset(idle[:], 0.0)
        nc.vector.memset(w_scales[:].bitcast(I32), 0)
        nc.vector.memset(bias_rows[0 : P - 1, :].bitcast(I32), 0)
        nc.vector.memset(warm[:], 0.0)
        nc.vector.memset(ones[:], 1.0)
        nc.vector.memset(half[:], 0.5)
        nc.vector.memset(norm_pad[:], 0.0)
        make_identity(nc, ident[:])
        nc.scalar.dma_start(out=bias_rows[P - 1 : P, :], in_=bq.unsqueeze(0))
        nc.scalar.activation(out=warm[:], in_=warm[:], func=ACT.Exp)

        def load_users(first, last):
            nc.sync.dma_start(
                out=x_sb[:, first:last, :],
                in_=cand_topics[first:last].rearrange("b n k -> n b k"),
            )

        load_users(0, FIRST)
        for quadrant in range(4):
            nc.sync.dma_start(
                out=w_scales[32 * quadrant : 32 * quadrant + 4, :].bitcast(I32),
                in_=Wq_scales[0, 4 * quadrant : 4 * quadrant + 4, :].bitcast(I32),
            )
        nc.sync.dma_start(out=w_words[:].bitcast(I32), in_=Wq_words[0].bitcast(I32))
        for first in range(FIRST, USERS, RATE):
            load_users(first, first + RATE)

        def transpose(users):
            xt = xt_pool.tile([P, users.stop - users.start, 2, P], F32, name="xt")
            for b in range(users.start, users.stop):
                words = x_sb[:, b, :].bitcast(F32)
                for u in range(2):
                    nc.tensor.transpose(xt[:, b - users.start, u, :], words[:, u : K // 2 : 2], ident[:])
            return xt

        def regroup(users, xt):
            nc.scalar.copy(
                out=grouped[:, users, :].bitcast(F32).rearrange("p b (r u) -> p b r u", u=2),
                in_=xt[:].rearrange("p b u r -> p b r u"),
            )

        def quantise(users):
            nc.vector.quantize_mx(
                out=x_codes[:, users, :].rearrange("p b r -> p (b r)").bitcast(FP8X4),
                scales=x_scales[:, users, :].rearrange("p b r -> p (b r)"),
                in_=grouped[:, users, :].rearrange("p b k -> p (b k)"),
            )

        def multiply(b, h):
            acc = acc_pool.tile([P, BANK], F32, name="acc")
            nc.tensor.matmul_mx(
                out=acc[:],
                lhsT=x_codes[:, b, :].bitcast(FP8X4),
                lhsT_scale=x_scales[:, b, :],
                rhs=w_words[:, 2 * BANK * h : 2 * BANK * (h + 1)].bitcast(FP4X4),
                rhs_scale=w_scales[:, BANK * h : BANK * (h + 1)],
                start=True,
                stop=True,
            )
            return acc

        def add_bias(h, acc, q_sb):
            cols = slice(BANK * h, BANK * (h + 1))
            nc.vector.tensor_tensor(out=q_sb[:, cols], in0=acc[:], in1=bias_sb[:, cols], op=ALU.add)

        def sum_squares(q_sb, cols, total):
            squares = squares_pool.tile([P, FEATURES], F32, name="squares")
            nc.scalar.activation(out=squares[:, cols], in_=q_sb[:, cols], func=ACT.Square, accum_out=total)

        def sum_squares_on_vector(q_sb, total):
            nc.vector.scalar_tensor_tensor(
                out=squares_v[:], in0=q_sb[:], scalar=1.0, in1=q_sb[:],
                op0=ALU.mult, op1=ALU.mult, accum_out=total,
            )

        def sums(first, last):
            tile = sum_early if first < USERS // 2 else sum_late
            start = first % (USERS // 2)
            return tile[:, start : start + last - first]

        def roots(first, last):
            users = slice(first, last)
            nc.gpsimd.tensor_tensor(
                out=norm_pad[:, users], in0=sums(first, last), in1=half[:, users], op=ALU.pow
            )

        idle_ps = acc_pool.tile([P, BANK], F32, name="acc")
        for i in range(WARM_UPS):
            nc.tensor.matmul(out=idle_ps[:, 0:P], lhsT=idle[:], rhs=idle[:], start=True, stop=True)

        for b in range(FIRST):
            regroup(slice(b, b + 1), transpose(slice(b, b + 1)))
        bias_ps = []
        for h in range(HALVES):
            cols = slice(BANK * h, BANK * (h + 1))
            half_ps = xt_pool.tile([P, BANK], BF16, name="bias_ps", tag="xt")
            nc.tensor.matmul(out=half_ps[:], lhsT=ones[:], rhs=bias_rows[:, cols], start=True, stop=True)
            bias_ps.append(half_ps)
        quantise(slice(0, 1))
        nc.vector.tensor_copy(out=bias_sb[:, 0:BANK], in_=bias_ps[0][:])
        nc.scalar.copy(out=bias_sb[:, BANK:FEATURES], in_=bias_ps[1][:])
        quantise(slice(1, 2))

        products = {0: [multiply(0, h) for h in range(HALVES)]}
        held = None
        idle_tail = None
        for b in range(USERS):
            if b == USERS - KEPT_WARM:
                idle_tail = xt_pool.tile([P, 2, P], F32, name="xt")[:, 0, :]
            q_sb = q_pool.tile([P, FEATURES], F32, name="q_sb")
            if b in QUANTISED:
                quantise(QUANTISED[b])
            if b in PREPARED and b != RELIEVED:
                regroup(PREPARED[b], transpose(PREPARED[b]))
            add_bias(0, products[b][0], q_sb)
            if b + 1 < USERS:
                products[b + 1] = [multiply(b + 1, h) for h in range(HALVES)]
            if b == RELIEVED:
                regroup(PREPARED[b], transpose(PREPARED[b]))
            if b + 1 == RELIEVED:
                nc.scalar.copy(out=y_half[:], in_=products[b + 1][1][:])
            if b == RELIEVED:
                cols = slice(BANK, FEATURES)
                nc.gpsimd.tensor_tensor(out=q_sb[:, cols], in0=y_half[:], in1=bias_sb[:, cols], op=ALU.add)
            else:
                add_bias(1, products[b][1], q_sb)
            nc.sync.dma_start(out=out_0[b], in_=q_sb[:])
            if b >= USERS - KEPT_WARM:
                for h in range(HALVES):
                    nc.tensor.matmul(
                        out=idle_tail[:, 0:P], lhsT=idle[:], rhs=q_sb[:, BANK * h : BANK * h + P], start=True, stop=True
                    )
            if b == 0:
                sum_squares(q_sb, slice(0, BANK), parts[:, 0:1])
                regroup(slice(3, 4), transpose(slice(3, 4)))
                sum_squares(q_sb, slice(BANK, FEATURES), parts[:, 1:2])
                nc.gpsimd.tensor_tensor(out=sums(0, 1), in0=parts[:, 0:1], in1=parts[:, 1:2], op=ALU.add)
            elif b == USERS - 2:
                held = q_sb
            else:
                sum_squares(q_sb, slice(0, FEATURES), sums(b, b + 1))
            if b == USERS - 1:
                sum_squares_on_vector(held, sums(b - 1, b))
            if b in ROOTS:
                roots(*ROOTS[b])

        norm_t = xt_pool.tile([P, 2, P], F32, name="xt")
        norms = norm_t[:, 0, :]
        nc.tensor.transpose(norms, norm_pad[:], ident[:])
        neg_max = keep.tile([P, 1], F32)
        expd = keep.tile([P, P], F32)
        total = keep.tile([P, 1], F32)
        inv_total = keep.tile([P, 1], F32)
        weights = keep.tile([P, P], F32)
        nc.vector.tensor_reduce(out=neg_max[:], in_=norms, axis=mybir.AxisListType.X, op=ALU.max, negate=True)
        nc.scalar.activation(out=expd[:], in_=norms, func=ACT.Exp, bias=neg_max[:], accum_out=total[:])
        nc.vector.reciprocal(out=inv_total[:], in_=total[:])
        nc.vector.tensor_scalar_mul(out=weights[:], in0=expd[:], scalar1=inv_total[:])
        nc.sync.dma_start(out=out_1, in_=weights[0:USERS, :])
